import numpy as np
import ml_dtypes

BF16 = ml_dtypes.bfloat16


def bf(x):
    return np.asarray(x, np.float32).astype(BF16)


def f32(x):
    return np.asarray(x, np.float32)


def f64(x):
    return np.asarray(x).astype(np.float64)


def striped(idx):
    return np.tile(idx.reshape(-1, 16).T, (8, 1))


S, D, F, M, H, K, N = 512, 128, 128, 256, 256, 8, 2048
EPS = 1e-5


def bn(v, gamma, beta):
    mean = v.mean(axis=1, keepdims=True)
    var = np.square(v - mean).mean(axis=1, keepdims=True)
    return (v - mean) / np.sqrt(var + EPS) * gamma + beta


def setup_inputs():
    table = bf(0.5 * np.random.standard_normal((1, D)) + (0.5 + np.random.random((1, D))) * np.random.standard_normal((S, D)))
    gamma_t = f32(0.25 * (1.0 + 0.2 * np.random.standard_normal((D, 1))))
    beta_t = f32(0.1 * np.random.standard_normal((D, 1)))
    w = bf(np.random.standard_normal((D, M)) / np.sqrt(D))
    fine = f32(0.5 * np.random.standard_normal((F, 1)) + (0.5 + np.random.random((F, 1))) * np.random.standard_normal((F, N)))
    gamma_f = f32(0.25 * (1.0 + 0.2 * np.random.standard_normal((F, 1))))
    beta_f = f32(0.1 * np.random.standard_normal((F, 1)))
    w_fine = bf(np.random.standard_normal((F, M)) / np.sqrt(F))
    idx = np.concatenate([np.random.permutation(S)[:H] for _ in range(K)])
    return {"table": table, "gamma_t": gamma_t, "beta_t": beta_t, "w": w, "fine": fine, "gamma_f": gamma_f, "beta_f": beta_f, "w_fine": w_fine, "offs": striped(idx)}


def reference(table, gamma_t, beta_t, w, fine, gamma_f, beta_f, w_fine, offs):
    idx = offs[:16].T.reshape(-1)
    tn = bn(f64(table).T, f64(gamma_t), f64(beta_t))
    fn = bn(f64(fine), f64(gamma_f), f64(beta_f))
    return f64(w).T @ tn[:, idx] + f64(w_fine).T @ fn

@@ -1,0 +1,100 @@
+import concourse.mybir as mybir
+from concourse.masks import make_identity
+
+BF16, F32, U16 = mybir.dt.bfloat16, mybir.dt.float32, mybir.dt.uint16
+MULT, SUBTRACT = mybir.AluOpType.mult, mybir.AluOpType.subtract
+SQRT = mybir.ActivationFunctionType.Sqrt
+
+P = 128
+S = 512
+M = 256
+N = 2048
+EPS = 1e-5
+PIECE = 512
+STATS = 6
+
+FLOPS = 2 * (P + P) * M * N
+
+
+def scale_and_shift(nc, pool, stats, gamma, beta, eps, label):
+    mean_var = pool.tile([P, 2], F32, name=label + "_mean_var")
+    nc.vector.bn_aggr(mean_var[:], stats)
+    std = pool.tile([P, 1], F32, name=label + "_std")
+    nc.scalar.activation(std[:], mean_var[:, 1:2], SQRT, bias=eps[:], scale=1.0)
+    rstd = pool.tile([P, 1], F32, name=label + "_rstd")
+    nc.vector.reciprocal(rstd[:], std[:])
+    scale = pool.tile([P, 1], F32, name=label + "_scale")
+    nc.vector.tensor_mul(scale[:], gamma[:], rstd[:])
+    shift = pool.tile([P, 1], F32, name=label + "_shift")
+    nc.vector.scalar_tensor_tensor(shift[:], mean_var[:, 0:1], scale[:], beta[:], op0=MULT, op1=SUBTRACT)
+    return scale, shift
+
+
+def tile_decoder_kernel(tc, table, gamma_t, beta_t, w, fine, gamma_f, beta_f, w_fine, offs, out):
+    nc = tc.nc
+    with (
+        tc.tile_pool(name="held", bufs=1) as held,
+        tc.tile_pool(name="staging", bufs=8) as staging,
+    ):
+        rows = held.tile([P, S // P, P], BF16, name="rows")
+        nc.sync.dma_start(rows[:], table.rearrange("(b p) d -> p b d", p=P))
+        offsets = held.tile([P, N // 16], U16, name="offsets")
+        nc.sync.dma_start(offsets[:], offs)
+        per_feature = {}
+        for label in ("gamma_t", "beta_t", "gamma_f", "beta_f"):
+            per_feature[label] = held.tile([P, 1], F32, name=label + "_sb")
+        nc.scalar.dma_start(per_feature["gamma_t"][:], gamma_t)
+        nc.scalar.dma_start(per_feature["beta_t"][:], beta_t)
+        w_sb = held.tile([P, M], BF16, name="w_sb")
+        nc.scalar.dma_start(w_sb[:], w)
+        fine_sb = [held.tile([P, PIECE], F32, name=f"fine_sb{j}") for j in range(N // PIECE)]
+        for j in range(N // PIECE):
+            queue = nc.sync if j % 2 == 0 else nc.scalar
+            queue.dma_start(fine_sb[j][:], fine[:, j * PIECE : (j + 1) * PIECE])
+        nc.sync.dma_start(per_feature["gamma_f"][:], gamma_f)
+        nc.scalar.dma_start(per_feature["beta_f"][:], beta_f)
+
+        identity = held.tile([P, P], BF16, name="identity")
+        make_identity(nc, identity[:])
+        w_fine_sb = held.tile([P, M], BF16, name="w_fine_sb")
+        nc.gpsimd.dma_start(w_fine_sb[:], w_fine)
+        eps = held.tile([P, 1], F32, name="eps")
+        nc.vector.memset(eps[:], EPS)
+
+        tn = held.tile([P, S], BF16, name="tn")
+        with tc.psum_pool(name="flip", bufs=1) as flip:
+            flipped = flip.tile([P, S], BF16, name="flipped")
+            for b in range(S // P):
+                nc.tensor.transpose(flipped[:, b * P : (b + 1) * P], rows[:, b, :], identity[:])
+            stats_t = held.tile([P, STATS], F32, name="stats_t")
+            nc.vector.bn_stats(stats_t[:], flipped[:])
+            scale_t, shift_t = scale_and_shift(
+                nc, held, stats_t[:], per_feature["gamma_t"], per_feature["beta_t"], eps, "t"
+            )
+            nc.vector.tensor_scalar(tn[:], flipped[:], scale_t[:], shift_t[:], op0=MULT, op1=SUBTRACT)
+
+        stats_f = held.tile([P, (N // PIECE) * STATS], F32, name="stats_f")
+        for j in range(N // PIECE):
+            nc.vector.bn_stats(stats_f[:, j * STATS : (j + 1) * STATS], fine_sb[j][:])
+        scale_f, shift_f = scale_and_shift(
+            nc, held, stats_f[:], per_feature["gamma_f"], per_feature["beta_f"], eps, "f"
+        )
+        fn = [held.tile([P, PIECE], BF16, name=f"fn{j}") for j in range(N // PIECE)]
+        for j in range(N // PIECE):
+            nc.vector.tensor_scalar(fn[j][:], fine_sb[j][:], scale_f[:], shift_f[:], op0=MULT, op1=SUBTRACT)
+
+        blocks = [(j, m) for j in range(N // PIECE) for m in range(M // P)]
+        with tc.psum_pool(name="banks", bufs=1) as banks:
+            bank = {}
+            for j, m in blocks:
+                bank[j, m] = banks.tile([P, PIECE], F32, name=f"bank{j}{m}")
+                picked = tn[:].indirect(offsets[:, j * (PIECE // 16) : (j + 1) * (PIECE // 16)])
+                nc.tensor.matmul(bank[j, m][:], w_sb[:, m * P : (m + 1) * P], picked, start=True, stop=False)
+            for j, m in blocks:
+                nc.tensor.matmul(bank[j, m][:], w_fine_sb[:, m * P : (m + 1) * P], fn[j][:], start=False, stop=True)
+                staged = staging.tile([P, PIECE], F32, name="staged")
+                if m == 0:
+                    nc.scalar.copy(staged[:], bank[j, m][:])
+                else:
+                    nc.vector.tensor_copy(staged[:], bank[j, m][:])
+                nc.sync.dma_start(out[m * P : (m + 1) * P, j * PIECE : (j + 1) * PIECE], staged[:])

@@ -2,8 +2,9 @@ import concourse.mybir as mybir
 from concourse.masks import make_identity
 
 BF16, F32, U16 = mybir.dt.bfloat16, mybir.dt.float32, mybir.dt.uint16
-MULT, SUBTRACT = mybir.AluOpType.mult, mybir.AluOpType.subtract
-SQRT = mybir.ActivationFunctionType.Sqrt
+MULT, SUBTRACT, POW = mybir.AluOpType.mult, mybir.AluOpType.subtract, mybir.AluOpType.pow
+IDENTITY = mybir.ActivationFunctionType.Identity
+RSQRT = mybir.ActivationFunctionType.Abs_reciprocal_sqrt
 
 P = 128
 S = 512
@@ -16,72 +17,76 @@ STATS = 6
 FLOPS = 2 * (P + P) * M * N
 
 
-def scale_and_shift(nc, pool, stats, gamma, beta, eps, label):
-    mean_var = pool.tile([P, 2], F32, name=label + "_mean_var")
-    nc.vector.bn_aggr(mean_var[:], stats)
-    std = pool.tile([P, 1], F32, name=label + "_std")
-    nc.scalar.activation(std[:], mean_var[:, 1:2], SQRT, bias=eps[:], scale=1.0)
-    rstd = pool.tile([P, 1], F32, name=label + "_rstd")
-    nc.vector.reciprocal(rstd[:], std[:])
-    scale = pool.tile([P, 1], F32, name=label + "_scale")
-    nc.vector.tensor_mul(scale[:], gamma[:], rstd[:])
-    shift = pool.tile([P, 1], F32, name=label + "_shift")
-    nc.vector.scalar_tensor_tensor(shift[:], mean_var[:, 0:1], scale[:], beta[:], op0=MULT, op1=SUBTRACT)
-    return scale, shift
-
-
 def tile_decoder_kernel(tc, table, gamma_t, beta_t, w, fine, gamma_f, beta_f, w_fine, offs, out):
     nc = tc.nc
     with (
         tc.tile_pool(name="held", bufs=1) as held,
         tc.tile_pool(name="staging", bufs=8) as staging,
+        tc.tile_pool(name="one_slot", bufs=1) as one_slot,
     ):
+        identity = held.tile([P, P], BF16, name="identity")
+        nc.vector.memset(identity[:], 0.0)
+        make_identity(nc, identity[:], nomemset=True)
+
         rows = held.tile([P, S // P, P], BF16, name="rows")
         nc.sync.dma_start(rows[:], table.rearrange("(b p) d -> p b d", p=P))
         offsets = held.tile([P, N // 16], U16, name="offsets")
         nc.sync.dma_start(offsets[:], offs)
-        per_feature = {}
-        for label in ("gamma_t", "beta_t", "gamma_f", "beta_f"):
-            per_feature[label] = held.tile([P, 1], F32, name=label + "_sb")
-        nc.scalar.dma_start(per_feature["gamma_t"][:], gamma_t)
-        nc.scalar.dma_start(per_feature["beta_t"][:], beta_t)
         w_sb = held.tile([P, M], BF16, name="w_sb")
-        nc.scalar.dma_start(w_sb[:], w)
-        fine_sb = [held.tile([P, PIECE], F32, name=f"fine_sb{j}") for j in range(N // PIECE)]
-        for j in range(N // PIECE):
-            queue = nc.sync if j % 2 == 0 else nc.scalar
-            queue.dma_start(fine_sb[j][:], fine[:, j * PIECE : (j + 1) * PIECE])
-        nc.sync.dma_start(per_feature["gamma_f"][:], gamma_f)
-        nc.scalar.dma_start(per_feature["beta_f"][:], beta_f)
+        nc.sync.dma_start(w_sb[:], w)
+        fine_sb = held.tile([P, N], F32, name="fine_sb")
+        nc.sync.dma_start(fine_sb[:], fine)
+        per_feature = {}
+        for label, vector in (("gamma_t", gamma_t), ("beta_t", beta_t), ("gamma_f", gamma_f), ("beta_f", beta_f)):
+            per_feature[label] = held.tile([P, 1], F32, name=label + "_sb")
+            nc.scalar.dma_start(per_feature[label][:], vector)
 
-        identity = held.tile([P, P], BF16, name="identity")
-        make_identity(nc, identity[:])
         w_fine_sb = held.tile([P, M], BF16, name="w_fine_sb")
         nc.gpsimd.dma_start(w_fine_sb[:], w_fine)
         eps = held.tile([P, 1], F32, name="eps")
         nc.vector.memset(eps[:], EPS)
+        minus_half = held.tile([P, 1], F32, name="minus_half")
+        nc.vector.memset(minus_half[:], -0.5)
 
         tn = held.tile([P, S], BF16, name="tn")
         with tc.psum_pool(name="flip", bufs=1) as flip:
             flipped = flip.tile([P, S], BF16, name="flipped")
             for b in range(S // P):
                 nc.tensor.transpose(flipped[:, b * P : (b + 1) * P], rows[:, b, :], identity[:])
-            stats_t = held.tile([P, STATS], F32, name="stats_t")
+            stats_t = one_slot.tile([P, STATS], F32, name="stats_t", tag="stats")
             nc.vector.bn_stats(stats_t[:], flipped[:])
-            scale_t, shift_t = scale_and_shift(
-                nc, held, stats_t[:], per_feature["gamma_t"], per_feature["beta_t"], eps, "t"
-            )
-            nc.vector.tensor_scalar(tn[:], flipped[:], scale_t[:], shift_t[:], op0=MULT, op1=SUBTRACT)
+            mean_var_t = held.tile([P, 2], F32, name="mean_var_t")
+            nc.vector.bn_aggr(mean_var_t[:], stats_t[:])
+            rstd_t = held.tile([P, 1], F32, name="rstd_t")
+            nc.scalar.activation(rstd_t[:], mean_var_t[:, 1:2], RSQRT, bias=eps[:], scale=1.0)
+            neg_mean_t = held.tile([P, 1], F32, name="neg_mean_t")
+            nc.scalar.activation(neg_mean_t[:], mean_var_t[:, 0:1], IDENTITY, scale=-1.0)
+            scale_t = held.tile([P, 1], F32, name="scale_t")
+            nc.scalar.activation(scale_t[:], rstd_t[:], IDENTITY, scale=per_feature["gamma_t"][:])
+            bias_t = held.tile([P, 1], F32, name="bias_t")
+            nc.scalar.activation(bias_t[:], neg_mean_t[:], IDENTITY, bias=per_feature["beta_t"][:], scale=scale_t[:])
+            nc.scalar.activation(tn[:], flipped[:], IDENTITY, bias=bias_t[:], scale=scale_t[:])
 
-        stats_f = held.tile([P, (N // PIECE) * STATS], F32, name="stats_f")
+        stats_f = one_slot.tile([P, (N // PIECE) * STATS], F32, name="stats_f", tag="stats")
         for j in range(N // PIECE):
-            nc.vector.bn_stats(stats_f[:, j * STATS : (j + 1) * STATS], fine_sb[j][:])
-        scale_f, shift_f = scale_and_shift(
-            nc, held, stats_f[:], per_feature["gamma_f"], per_feature["beta_f"], eps, "f"
+            nc.vector.bn_stats(stats_f[:, j * STATS : (j + 1) * STATS], fine_sb[:, j * PIECE : (j + 1) * PIECE])
+        mean_var_f = held.tile([P, 2], F32, name="mean_var_f")
+        nc.vector.bn_aggr(mean_var_f[:], stats_f[:])
+        var_eps_f = held.tile([P, 1], F32, name="var_eps_f")
+        nc.vector.tensor_scalar_add(var_eps_f[:], mean_var_f[:, 1:2], EPS)
+        rstd_f = held.tile([P, 1], F32, name="rstd_f")
+        nc.gpsimd.tensor_tensor(rstd_f[:], var_eps_f[:], minus_half[:], POW)
+        scale_f = held.tile([P, 1], F32, name="scale_f")
+        nc.vector.tensor_mul(scale_f[:], per_feature["gamma_f"][:], rstd_f[:])
+        shift_f = held.tile([P, 1], F32, name="shift_f")
+        nc.vector.scalar_tensor_tensor(
+            shift_f[:], mean_var_f[:, 0:1], scale_f[:], per_feature["beta_f"][:], op0=MULT, op1=SUBTRACT
         )
         fn = [held.tile([P, PIECE], BF16, name=f"fn{j}") for j in range(N // PIECE)]
         for j in range(N // PIECE):
-            nc.vector.tensor_scalar(fn[j][:], fine_sb[j][:], scale_f[:], shift_f[:], op0=MULT, op1=SUBTRACT)
+            nc.vector.tensor_scalar(
+                fn[j][:], fine_sb[:, j * PIECE : (j + 1) * PIECE], scale_f[:], shift_f[:], op0=MULT, op1=SUBTRACT
+            )
 
         blocks = [(j, m) for j in range(N // PIECE) for m in range(M // P)]
         with tc.psum_pool(name="banks", bufs=1) as banks:

@@ -13,6 +13,7 @@ N = 2048
 EPS = 1e-5
 PIECE = 512
 STATS = 6
+WARM_UP = 4
 
 FLOPS = 2 * (P + P) * M * N
 
@@ -53,19 +54,20 @@ def tile_decoder_kernel(tc, table, gamma_t, beta_t, w, fine, gamma_f, beta_f, w_
             flipped = flip.tile([P, S], BF16, name="flipped")
             for b in range(S // P):
                 nc.tensor.transpose(flipped[:, b * P : (b + 1) * P], rows[:, b, :], identity[:])
+            unread = flip.tile([P, S], F32, name="unread")
+            for turn in range(WARM_UP):
+                nc.tensor.matmul(unread[:], identity[:], rows[:].rearrange("p b d -> p (b d)"), start=True, stop=True)
             stats_t = one_slot.tile([P, STATS], F32, name="stats_t", tag="stats")
             nc.vector.bn_stats(stats_t[:], flipped[:])
             mean_var_t = held.tile([P, 2], F32, name="mean_var_t")
             nc.vector.bn_aggr(mean_var_t[:], stats_t[:])
-            rstd_t = held.tile([P, 1], F32, name="rstd_t")
-            nc.scalar.activation(rstd_t[:], mean_var_t[:, 1:2], RSQRT, bias=eps[:], scale=1.0)
-            neg_mean_t = held.tile([P, 1], F32, name="neg_mean_t")
-            nc.scalar.activation(neg_mean_t[:], mean_var_t[:, 0:1], IDENTITY, scale=-1.0)
-            scale_t = held.tile([P, 1], F32, name="scale_t")
-            nc.scalar.activation(scale_t[:], rstd_t[:], IDENTITY, scale=per_feature["gamma_t"][:])
-            bias_t = held.tile([P, 1], F32, name="bias_t")
-            nc.scalar.activation(bias_t[:], neg_mean_t[:], IDENTITY, bias=per_feature["beta_t"][:], scale=scale_t[:])
-            nc.scalar.activation(tn[:], flipped[:], IDENTITY, bias=bias_t[:], scale=scale_t[:])
+            centred = held.tile([P, S], F32, name="centred")
+            nc.vector.tensor_scalar_sub(centred[:], flipped[:], mean_var_t[:, 0:1])
+        rstd_t = held.tile([P, 1], F32, name="rstd_t")
+        nc.scalar.activation(rstd_t[:], mean_var_t[:, 1:2], RSQRT, bias=eps[:], scale=1.0)
+        scale_t = held.tile([P, 1], F32, name="scale_t")
+        nc.scalar.activation(scale_t[:], rstd_t[:], IDENTITY, scale=per_feature["gamma_t"][:])
+        nc.scalar.activation(tn[:], centred[:], IDENTITY, bias=per_feature["beta_t"][:], scale=scale_t[:])
 
         stats_f = one_slot.tile([P, (N // PIECE) * STATS], F32, name="stats_f", tag="stats")
         for j in range(N // PIECE):

@@ -2,7 +2,7 @@ import concourse.mybir as mybir
 from concourse.masks import make_identity
 
 BF16, F32, U16 = mybir.dt.bfloat16, mybir.dt.float32, mybir.dt.uint16
-MULT, SUBTRACT, POW = mybir.AluOpType.mult, mybir.AluOpType.subtract, mybir.AluOpType.pow
+MULT, ADD = mybir.AluOpType.mult, mybir.AluOpType.add
 IDENTITY = mybir.ActivationFunctionType.Identity
 RSQRT = mybir.ActivationFunctionType.Abs_reciprocal_sqrt
 
@@ -12,10 +12,24 @@ M = 256
 N = 2048
 EPS = 1e-5
 PIECE = 512
+HALF = S // 2
 STATS = 6
 WARM_UP = 4
 
 FLOPS = 2 * (P + P) * M * N
+
+
+def scale_and_bias(nc, pool, stats, gamma, beta, eps, bias, label):
+    mean_var = pool.tile([P, 2], F32, name="mean_var_" + label)
+    nc.vector.bn_aggr(mean_var[:], stats)
+    rstd = pool.tile([P, 1], F32, name="rstd_" + label)
+    nc.scalar.activation(rstd[:], mean_var[:, 1:2], RSQRT, bias=eps[:], scale=1.0)
+    neg_mean = pool.tile([P, 1], F32, name="neg_mean_" + label)
+    nc.vector.tensor_scalar_mul(neg_mean[:], mean_var[:, 0:1], -1.0)
+    scale = pool.tile([P, 1], F32, name="scale_" + label)
+    nc.vector.tensor_mul(scale[:], gamma, rstd[:])
+    nc.vector.scalar_tensor_tensor(bias, neg_mean[:], scale[:], beta, op0=MULT, op1=ADD)
+    return scale
 
 
 def tile_decoder_kernel(tc, table, gamma_t, beta_t, w, fine, gamma_f, beta_f, w_fine, offs, out):
@@ -46,48 +60,38 @@ def tile_decoder_kernel(tc, table, gamma_t, beta_t, w, fine, gamma_f, beta_f, w_
         nc.gpsimd.dma_start(w_fine_sb[:], w_fine)
         eps = held.tile([P, 1], F32, name="eps")
         nc.vector.memset(eps[:], EPS)
-        minus_half = held.tile([P, 1], F32, name="minus_half")
-        nc.vector.memset(minus_half[:], -0.5)
 
         tn = held.tile([P, S], BF16, name="tn")
         with tc.psum_pool(name="flip", bufs=1) as flip:
-            flipped = flip.tile([P, S], BF16, name="flipped")
-            for b in range(S // P):
-                nc.tensor.transpose(flipped[:, b * P : (b + 1) * P], rows[:, b, :], identity[:])
+            flipped = [flip.tile([P, HALF], BF16, name=f"flipped{h}") for h in range(2)]
+            stats_t = held.tile([P, 2 * STATS], F32, name="stats_t")
+            for h in range(2):
+                for b in range(HALF // P):
+                    nc.tensor.transpose(
+                        flipped[h][:, b * P : (b + 1) * P], rows[:, h * (HALF // P) + b, :], identity[:]
+                    )
+                nc.vector.bn_stats(stats_t[:, h * STATS : (h + 1) * STATS], flipped[h][:])
             unread = flip.tile([P, S], F32, name="unread")
             for turn in range(WARM_UP):
                 nc.tensor.matmul(unread[:], identity[:], rows[:].rearrange("p b d -> p (b d)"), start=True, stop=True)
-            stats_t = one_slot.tile([P, STATS], F32, name="stats_t", tag="stats")
-            nc.vector.bn_stats(stats_t[:], flipped[:])
-            mean_var_t = held.tile([P, 2], F32, name="mean_var_t")
-            nc.vector.bn_aggr(mean_var_t[:], stats_t[:])
-            centred = held.tile([P, S], F32, name="centred")
-            nc.vector.tensor_scalar_sub(centred[:], flipped[:], mean_var_t[:, 0:1])
-        rstd_t = held.tile([P, 1], F32, name="rstd_t")
-        nc.scalar.activation(rstd_t[:], mean_var_t[:, 1:2], RSQRT, bias=eps[:], scale=1.0)
-        scale_t = held.tile([P, 1], F32, name="scale_t")
-        nc.scalar.activation(scale_t[:], rstd_t[:], IDENTITY, scale=per_feature["gamma_t"][:])
-        nc.scalar.activation(tn[:], centred[:], IDENTITY, bias=per_feature["beta_t"][:], scale=scale_t[:])
+            bias_t = one_slot.tile([P, 1], F32, name="bias_t", tag="handover")
+            scale_t = scale_and_bias(
+                nc, held, stats_t[:], per_feature["gamma_t"][:], per_feature["beta_t"][:], eps, bias_t[:], "t"
+            )
+            nc.scalar.activation(tn[:, 0:HALF], flipped[0][:], IDENTITY, bias=bias_t[:], scale=scale_t[:])
+            nc.vector.tensor_scalar(tn[:, HALF:S], flipped[1][:], scale_t[:], bias_t[:], op0=MULT, op1=ADD)
 
-        stats_f = one_slot.tile([P, (N // PIECE) * STATS], F32, name="stats_f", tag="stats")
+        stats_f = one_slot.tile([P, (N // PIECE) * STATS], F32, name="stats_f", tag="handover")
         for j in range(N // PIECE):
             nc.vector.bn_stats(stats_f[:, j * STATS : (j + 1) * STATS], fine_sb[:, j * PIECE : (j + 1) * PIECE])
-        mean_var_f = held.tile([P, 2], F32, name="mean_var_f")
-        nc.vector.bn_aggr(mean_var_f[:], stats_f[:])
-        var_eps_f = held.tile([P, 1], F32, name="var_eps_f")
-        nc.vector.tensor_scalar_add(var_eps_f[:], mean_var_f[:, 1:2], EPS)
-        rstd_f = held.tile([P, 1], F32, name="rstd_f")
-        nc.gpsimd.tensor_tensor(rstd_f[:], var_eps_f[:], minus_half[:], POW)
-        scale_f = held.tile([P, 1], F32, name="scale_f")
-        nc.vector.tensor_mul(scale_f[:], per_feature["gamma_f"][:], rstd_f[:])
-        shift_f = held.tile([P, 1], F32, name="shift_f")
-        nc.vector.scalar_tensor_tensor(
-            shift_f[:], mean_var_f[:, 0:1], scale_f[:], per_feature["beta_f"][:], op0=MULT, op1=SUBTRACT
+        bias_f = held.tile([P, 1], F32, name="bias_f")
+        scale_f = scale_and_bias(
+            nc, held, stats_f[:], per_feature["gamma_f"][:], per_feature["beta_f"][:], eps, bias_f[:], "f"
         )
         fn = [held.tile([P, PIECE], BF16, name=f"fn{j}") for j in range(N // PIECE)]
         for j in range(N // PIECE):
             nc.vector.tensor_scalar(
-                fn[j][:], fine_sb[:, j * PIECE : (j + 1) * PIECE], scale_f[:], shift_f[:], op0=MULT, op1=SUBTRACT
+                fn[j][:], fine_sb[:, j * PIECE : (j + 1) * PIECE], scale_f[:], bias_f[:], op0=MULT, op1=ADD
             )
 
         blocks = [(j, m) for j in range(N // PIECE) for m in range(M // P)]

@@ -14,7 +14,6 @@ EPS = 1e-5
 PIECE = 512
 HALF = S // 2
 STATS = 6
-WARM_UP = 4
 
 FLOPS = 2 * (P + P) * M * N
 
@@ -71,9 +70,6 @@ def tile_decoder_kernel(tc, table, gamma_t, beta_t, w, fine, gamma_f, beta_f, w_
                         flipped[h][:, b * P : (b + 1) * P], rows[:, h * (HALF // P) + b, :], identity[:]
                     )
                 nc.vector.bn_stats(stats_t[:, h * STATS : (h + 1) * STATS], flipped[h][:])
-            unread = flip.tile([P, S], F32, name="unread")
-            for turn in range(WARM_UP):
-                nc.tensor.matmul(unread[:], identity[:], rows[:].rearrange("p b d -> p (b d)"), start=True, stop=True)
             bias_t = one_slot.tile([P, 1], F32, name="bias_t", tag="handover")
             scale_t = scale_and_bias(
                 nc, held, stats_t[:], per_feature["gamma_t"][:], per_feature["beta_t"][:], eps, bias_t[:], "t"

@@ -3,7 +3,6 @@ from concourse.masks import make_identity
 
 BF16, F32, U16 = mybir.dt.bfloat16, mybir.dt.float32, mybir.dt.uint16
 MULT, ADD = mybir.AluOpType.mult, mybir.AluOpType.add
-IDENTITY = mybir.ActivationFunctionType.Identity
 RSQRT = mybir.ActivationFunctionType.Abs_reciprocal_sqrt
 
 P = 128
@@ -18,14 +17,14 @@ STATS = 6
 FLOPS = 2 * (P + P) * M * N
 
 
-def scale_and_bias(nc, pool, stats, gamma, beta, eps, bias, label):
-    mean_var = pool.tile([P, 2], F32, name="mean_var_" + label)
+def scale_and_bias(nc, pool, stats, gamma, beta, eps, bias, level):
+    mean_var = pool.tile([P, 2], F32, name="mean_var_" + level)
     nc.vector.bn_aggr(mean_var[:], stats)
-    rstd = pool.tile([P, 1], F32, name="rstd_" + label)
+    rstd = pool.tile([P, 1], F32, name="rstd_" + level)
     nc.scalar.activation(rstd[:], mean_var[:, 1:2], RSQRT, bias=eps[:], scale=1.0)
-    neg_mean = pool.tile([P, 1], F32, name="neg_mean_" + label)
+    neg_mean = pool.tile([P, 1], F32, name="neg_mean_" + level)
     nc.vector.tensor_scalar_mul(neg_mean[:], mean_var[:, 0:1], -1.0)
-    scale = pool.tile([P, 1], F32, name="scale_" + label)
+    scale = pool.tile([P, 1], F32, name="scale_" + level)
     nc.vector.tensor_mul(scale[:], gamma, rstd[:])
     nc.vector.scalar_tensor_tensor(bias, neg_mean[:], scale[:], beta, op0=MULT, op1=ADD)
     return scale
@@ -35,15 +34,17 @@ def tile_decoder_kernel(tc, table, gamma_t, beta_t, w, fine, gamma_f, beta_f, w_
     nc = tc.nc
     with (
         tc.tile_pool(name="held", bufs=1) as held,
-        tc.tile_pool(name="staging", bufs=8) as staging,
-        tc.tile_pool(name="one_slot", bufs=1) as one_slot,
+        tc.tile_pool(name="handover", bufs=1) as handover,
+        tc.tile_pool(name="staging", bufs=(N // PIECE) * (M // P)) as staging,
     ):
         identity = held.tile([P, P], BF16, name="identity")
         nc.vector.memset(identity[:], 0.0)
         make_identity(nc, identity[:], nomemset=True)
+        eps = held.tile([P, 1], F32, name="eps")
+        nc.vector.memset(eps[:], EPS)
 
         rows = held.tile([P, S // P, P], BF16, name="rows")
-        nc.sync.dma_start(rows[:], table.rearrange("(b p) d -> p b d", p=P))
+        nc.sync.dma_start(rows[:], table.rearrange("(r p) d -> p r d", p=P))
         offsets = held.tile([P, N // 16], U16, name="offsets")
         nc.sync.dma_start(offsets[:], offs)
         w_sb = held.tile([P, M], BF16, name="w_sb")
@@ -54,30 +55,29 @@ def tile_decoder_kernel(tc, table, gamma_t, beta_t, w, fine, gamma_f, beta_f, w_
         for label, vector in (("gamma_t", gamma_t), ("beta_t", beta_t), ("gamma_f", gamma_f), ("beta_f", beta_f)):
             per_feature[label] = held.tile([P, 1], F32, name=label + "_sb")
             nc.scalar.dma_start(per_feature[label][:], vector)
-
         w_fine_sb = held.tile([P, M], BF16, name="w_fine_sb")
         nc.gpsimd.dma_start(w_fine_sb[:], w_fine)
-        eps = held.tile([P, 1], F32, name="eps")
-        nc.vector.memset(eps[:], EPS)
 
         tn = held.tile([P, S], BF16, name="tn")
         with tc.psum_pool(name="flip", bufs=1) as flip:
             flipped = [flip.tile([P, HALF], BF16, name=f"flipped{h}") for h in range(2)]
             stats_t = held.tile([P, 2 * STATS], F32, name="stats_t")
             for h in range(2):
-                for b in range(HALF // P):
+                for r in range(HALF // P):
                     nc.tensor.transpose(
-                        flipped[h][:, b * P : (b + 1) * P], rows[:, h * (HALF // P) + b, :], identity[:]
+                        flipped[h][:, r * P : (r + 1) * P], rows[:, h * (HALF // P) + r, :], identity[:]
                     )
                 nc.vector.bn_stats(stats_t[:, h * STATS : (h + 1) * STATS], flipped[h][:])
-            bias_t = one_slot.tile([P, 1], F32, name="bias_t", tag="handover")
+            bias_t = handover.tile([P, 1], F32, name="bias_t", tag="slot")
             scale_t = scale_and_bias(
                 nc, held, stats_t[:], per_feature["gamma_t"][:], per_feature["beta_t"][:], eps, bias_t[:], "t"
             )
-            nc.scalar.activation(tn[:, 0:HALF], flipped[0][:], IDENTITY, bias=bias_t[:], scale=scale_t[:])
-            nc.vector.tensor_scalar(tn[:, HALF:S], flipped[1][:], scale_t[:], bias_t[:], op0=MULT, op1=ADD)
+            for h in range(2):
+                nc.vector.tensor_scalar(
+                    tn[:, h * HALF : (h + 1) * HALF], flipped[h][:], scale_t[:], bias_t[:], op0=MULT, op1=ADD
+                )
 
-        stats_f = one_slot.tile([P, (N // PIECE) * STATS], F32, name="stats_f", tag="handover")
+        stats_f = handover.tile([P, (N // PIECE) * STATS], F32, name="stats_f", tag="slot")
         for j in range(N // PIECE):
             nc.vector.bn_stats(stats_f[:, j * STATS : (j + 1) * STATS], fine_sb[:, j * PIECE : (j + 1) * PIECE])
         bias_f = held.tile([P, 1], F32, name="bias_f")
@@ -90,14 +90,14 @@ def tile_decoder_kernel(tc, table, gamma_t, beta_t, w, fine, gamma_f, beta_f, w_
                 fn[j][:], fine_sb[:, j * PIECE : (j + 1) * PIECE], scale_f[:], bias_f[:], op0=MULT, op1=ADD
             )
 
-        blocks = [(j, m) for j in range(N // PIECE) for m in range(M // P)]
+        corners = [(j, m) for j in range(N // PIECE) for m in range(M // P)]
         with tc.psum_pool(name="banks", bufs=1) as banks:
             bank = {}
-            for j, m in blocks:
+            for j, m in corners:
                 bank[j, m] = banks.tile([P, PIECE], F32, name=f"bank{j}{m}")
                 picked = tn[:].indirect(offsets[:, j * (PIECE // 16) : (j + 1) * (PIECE // 16)])
                 nc.tensor.matmul(bank[j, m][:], w_sb[:, m * P : (m + 1) * P], picked, start=True, stop=False)
-            for j, m in blocks:
+            for j, m in corners:
                 nc.tensor.matmul(bank[j, m][:], w_fine_sb[:, m * P : (m + 1) * P], fn[j][:], start=False, stop=True)
                 staged = staging.tile([P, PIECE], F32, name="staged")
                 if m == 0:

@@ -12,6 +12,7 @@ N = 2048
 EPS = 1e-5
 PIECE = 512
 HALF = S // 2
+SLICE = 128
 STATS = 6
 
 FLOPS = 2 * (P + P) * M * N
@@ -90,18 +91,32 @@ def tile_decoder_kernel(tc, table, gamma_t, beta_t, w, fine, gamma_f, beta_f, w_
                 fn[j][:], fine_sb[:, j * PIECE : (j + 1) * PIECE], scale_f[:], bias_f[:], op0=MULT, op1=ADD
             )
 
-        corners = [(j, m) for j in range(N // PIECE) for m in range(M // P)]
+        def open_bank(j, m):
+            bank[j, m] = banks.tile([P, PIECE], F32, name=f"bank{j}{m}", tag=f"bank{j % 3}{m}")
+            picked = tn[:].indirect(offsets[:, j * (PIECE // 16) : (j + 1) * (PIECE // 16)])
+            nc.tensor.matmul(bank[j, m][:], w_sb[:, m * P : (m + 1) * P], picked, start=True, stop=False)
+
+        def close_bank(j, m):
+            for c in range(0, PIECE, SLICE):
+                nc.tensor.matmul(
+                    bank[j, m][:, c : c + SLICE],
+                    w_fine_sb[:, m * P : (m + 1) * P],
+                    fn[j][:, c : c + SLICE],
+                    start=False,
+                    stop=(c + SLICE == PIECE),
+                )
+            staged = staging.tile([P, PIECE], F32, name="staged")
+            if m == 0:
+                nc.scalar.copy(staged[:], bank[j, m][:])
+            else:
+                nc.vector.tensor_copy(staged[:], bank[j, m][:])
+            nc.sync.dma_start(out[m * P : (m + 1) * P, j * PIECE : (j + 1) * PIECE], staged[:])
+
+        runs = [[(j, m) for j in range(0, 3) for m in range(M // P)], [(3, m) for m in range(M // P)]]
         with tc.psum_pool(name="banks", bufs=1) as banks:
             bank = {}
-            for j, m in corners:
-                bank[j, m] = banks.tile([P, PIECE], F32, name=f"bank{j}{m}")
-                picked = tn[:].indirect(offsets[:, j * (PIECE // 16) : (j + 1) * (PIECE // 16)])
-                nc.tensor.matmul(bank[j, m][:], w_sb[:, m * P : (m + 1) * P], picked, start=True, stop=False)
-            for j, m in corners:
-                nc.tensor.matmul(bank[j, m][:], w_fine_sb[:, m * P : (m + 1) * P], fn[j][:], start=False, stop=True)
-                staged = staging.tile([P, PIECE], F32, name="staged")
-                if m == 0:
-                    nc.scalar.copy(staged[:], bank[j, m][:])
-                else:
-                    nc.vector.tensor_copy(staged[:], bank[j, m][:])
-                nc.sync.dma_start(out[m * P : (m + 1) * P, j * PIECE : (j + 1) * PIECE], staged[:])
+            for corners in runs:
+                for j, m in corners:
+                    open_bank(j, m)
+                for j, m in corners:
+                    close_bank(j, m)

@@ -4,6 +4,7 @@ from concourse.masks import make_identity
 BF16, F32, U16 = mybir.dt.bfloat16, mybir.dt.float32, mybir.dt.uint16
 MULT, ADD = mybir.AluOpType.mult, mybir.AluOpType.add
 RSQRT = mybir.ActivationFunctionType.Abs_reciprocal_sqrt
+IDENTITY, COPY = mybir.ActivationFunctionType.Identity, mybir.ActivationFunctionType.Copy
 
 P = 128
 S = 512
@@ -18,17 +19,13 @@ STATS = 6
 FLOPS = 2 * (P + P) * M * N
 
 
-def scale_and_bias(nc, pool, stats, gamma, beta, eps, bias, level):
-    mean_var = pool.tile([P, 2], F32, name="mean_var_" + level)
+def mean_and_rstd(nc, pool, mean_var, stats, eps, level):
     nc.vector.bn_aggr(mean_var[:], stats)
     rstd = pool.tile([P, 1], F32, name="rstd_" + level)
     nc.scalar.activation(rstd[:], mean_var[:, 1:2], RSQRT, bias=eps[:], scale=1.0)
     neg_mean = pool.tile([P, 1], F32, name="neg_mean_" + level)
     nc.vector.tensor_scalar_mul(neg_mean[:], mean_var[:, 0:1], -1.0)
-    scale = pool.tile([P, 1], F32, name="scale_" + level)
-    nc.vector.tensor_mul(scale[:], gamma, rstd[:])
-    nc.vector.scalar_tensor_tensor(bias, neg_mean[:], scale[:], beta, op0=MULT, op1=ADD)
-    return scale
+    return neg_mean, rstd
 
 
 def tile_decoder_kernel(tc, table, gamma_t, beta_t, w, fine, gamma_f, beta_f, w_fine, offs, out):
@@ -69,21 +66,27 @@ def tile_decoder_kernel(tc, table, gamma_t, beta_t, w, fine, gamma_f, beta_f, w_
                         flipped[h][:, r * P : (r + 1) * P], rows[:, h * (HALF // P) + r, :], identity[:]
                     )
                 nc.vector.bn_stats(stats_t[:, h * STATS : (h + 1) * STATS], flipped[h][:])
-            bias_t = handover.tile([P, 1], F32, name="bias_t", tag="slot")
-            scale_t = scale_and_bias(
-                nc, held, stats_t[:], per_feature["gamma_t"][:], per_feature["beta_t"][:], eps, bias_t[:], "t"
-            )
+            mean_var_t = handover.tile([P, 2], F32, name="mean_var_t", tag="slot")
+            neg_mean_t, rstd_t = mean_and_rstd(nc, held, mean_var_t, stats_t[:], eps, "t")
+            scale_t = held.tile([P, 1], F32, name="scale_t")
+            nc.scalar.activation(scale_t[:], rstd_t[:], COPY, scale=per_feature["gamma_t"][:])
+            bias_t = held.tile([P, 1], F32, name="bias_t")
+            nc.scalar.activation(bias_t[:], neg_mean_t[:], IDENTITY, bias=per_feature["beta_t"][:], scale=scale_t[:])
             for h in range(2):
-                nc.vector.tensor_scalar(
-                    tn[:, h * HALF : (h + 1) * HALF], flipped[h][:], scale_t[:], bias_t[:], op0=MULT, op1=ADD
+                nc.scalar.activation(
+                    tn[:, h * HALF : (h + 1) * HALF], flipped[h][:], IDENTITY, bias=bias_t[:], scale=scale_t[:]
                 )
 
         stats_f = handover.tile([P, (N // PIECE) * STATS], F32, name="stats_f", tag="slot")
         for j in range(N // PIECE):
             nc.vector.bn_stats(stats_f[:, j * STATS : (j + 1) * STATS], fine_sb[:, j * PIECE : (j + 1) * PIECE])
+        mean_var_f = held.tile([P, 2], F32, name="mean_var_f")
+        neg_mean_f, rstd_f = mean_and_rstd(nc, held, mean_var_f, stats_f[:], eps, "f")
+        scale_f = held.tile([P, 1], F32, name="scale_f")
+        nc.vector.tensor_mul(scale_f[:], per_feature["gamma_f"][:], rstd_f[:])
         bias_f = held.tile([P, 1], F32, name="bias_f")
-        scale_f = scale_and_bias(
-            nc, held, stats_f[:], per_feature["gamma_f"][:], per_feature["beta_f"][:], eps, bias_f[:], "f"
+        nc.vector.scalar_tensor_tensor(
+            bias_f[:], neg_mean_f[:], scale_f[:], per_feature["beta_f"][:], op0=MULT, op1=ADD
         )
         fn = [held.tile([P, PIECE], BF16, name=f"fn{j}") for j in range(N // PIECE)]
         for j in range(N // PIECE):

@@ -19,13 +19,13 @@ STATS = 6
 FLOPS = 2 * (P + P) * M * N
 
 
-def mean_and_rstd(nc, pool, mean_var, stats, eps, level):
+def mean_and_rstd(nc, pool, rstd, stats, eps, minus_one, level):
+    mean_var = pool.tile([P, 2], F32, name="mean_var_" + level)
     nc.vector.bn_aggr(mean_var[:], stats)
-    rstd = pool.tile([P, 1], F32, name="rstd_" + level)
     nc.scalar.activation(rstd[:], mean_var[:, 1:2], RSQRT, bias=eps[:], scale=1.0)
     neg_mean = pool.tile([P, 1], F32, name="neg_mean_" + level)
-    nc.vector.tensor_scalar_mul(neg_mean[:], mean_var[:, 0:1], -1.0)
-    return neg_mean, rstd
+    nc.vector.tensor_scalar_mul(neg_mean[:], mean_var[:, 0:1], minus_one)
+    return neg_mean
 
 
 def tile_decoder_kernel(tc, table, gamma_t, beta_t, w, fine, gamma_f, beta_f, w_fine, offs, out):
@@ -40,19 +40,27 @@ def tile_decoder_kernel(tc, table, gamma_t, beta_t, w, fine, gamma_f, beta_f, w_
         make_identity(nc, identity[:], nomemset=True)
         eps = held.tile([P, 1], F32, name="eps")
         nc.vector.memset(eps[:], EPS)
+        minus_one_t = handover.tile([P, 1], F32, name="minus_one_t", tag="slot")
+        nc.vector.memset(minus_one_t[:], -1.0)
 
         rows = held.tile([P, S // P, P], BF16, name="rows")
         nc.sync.dma_start(rows[:], table.rearrange("(r p) d -> p r d", p=P))
+        fine_sb = held.tile([P, N], F32, name="fine_sb")
+        for first, last in ((0, PIECE), (PIECE, 2 * PIECE), (2 * PIECE, N)):
+            nc.sync.dma_start(fine_sb[:, first:last], fine[:, first:last])
         offsets = held.tile([P, N // 16], U16, name="offsets")
         nc.sync.dma_start(offsets[:], offs)
         w_sb = held.tile([P, M], BF16, name="w_sb")
         nc.sync.dma_start(w_sb[:], w)
-        fine_sb = held.tile([P, N], F32, name="fine_sb")
-        nc.sync.dma_start(fine_sb[:], fine)
         per_feature = {}
-        for label, vector in (("gamma_t", gamma_t), ("beta_t", beta_t), ("gamma_f", gamma_f), ("beta_f", beta_f)):
+        for label, vector, queue in (
+            ("gamma_t", gamma_t, nc.scalar),
+            ("beta_t", beta_t, nc.scalar),
+            ("gamma_f", gamma_f, nc.gpsimd),
+            ("beta_f", beta_f, nc.gpsimd),
+        ):
             per_feature[label] = held.tile([P, 1], F32, name=label + "_sb")
-            nc.scalar.dma_start(per_feature[label][:], vector)
+            queue.dma_start(per_feature[label][:], vector)
         w_fine_sb = held.tile([P, M], BF16, name="w_fine_sb")
         nc.gpsimd.dma_start(w_fine_sb[:], w_fine)
 
@@ -66,11 +74,11 @@ def tile_decoder_kernel(tc, table, gamma_t, beta_t, w, fine, gamma_f, beta_f, w_
                         flipped[h][:, r * P : (r + 1) * P], rows[:, h * (HALF // P) + r, :], identity[:]
                     )
                 nc.vector.bn_stats(stats_t[:, h * STATS : (h + 1) * STATS], flipped[h][:])
-            mean_var_t = handover.tile([P, 2], F32, name="mean_var_t", tag="slot")
-            neg_mean_t, rstd_t = mean_and_rstd(nc, held, mean_var_t, stats_t[:], eps, "t")
+            rstd_t = held.tile([P, 1], F32, name="rstd_t")
+            neg_mean_t = mean_and_rstd(nc, held, rstd_t, stats_t[:], eps, minus_one_t[:], "t")
             scale_t = held.tile([P, 1], F32, name="scale_t")
             nc.scalar.activation(scale_t[:], rstd_t[:], COPY, scale=per_feature["gamma_t"][:])
-            bias_t = held.tile([P, 1], F32, name="bias_t")
+            bias_t = handover.tile([P, 1], F32, name="bias_t", tag="scalar_slot")
             nc.scalar.activation(bias_t[:], neg_mean_t[:], IDENTITY, bias=per_feature["beta_t"][:], scale=scale_t[:])
             for h in range(2):
                 nc.scalar.activation(
@@ -80,8 +88,8 @@ def tile_decoder_kernel(tc, table, gamma_t, beta_t, w, fine, gamma_f, beta_f, w_
         stats_f = handover.tile([P, (N // PIECE) * STATS], F32, name="stats_f", tag="slot")
         for j in range(N // PIECE):
             nc.vector.bn_stats(stats_f[:, j * STATS : (j + 1) * STATS], fine_sb[:, j * PIECE : (j + 1) * PIECE])
-        mean_var_f = held.tile([P, 2], F32, name="mean_var_f")
-        neg_mean_f, rstd_f = mean_and_rstd(nc, held, mean_var_f, stats_f[:], eps, "f")
+        rstd_f = handover.tile([P, 1], F32, name="rstd_f", tag="scalar_slot")
+        neg_mean_f = mean_and_rstd(nc, held, rstd_f, stats_f[:], eps, -1.0, "f")
         scale_f = held.tile([P, 1], F32, name="scale_f")
         nc.vector.tensor_mul(scale_f[:], per_feature["gamma_f"][:], rstd_f[:])
         bias_f = held.tile([P, 1], F32, name="bias_f")
@@ -94,20 +102,23 @@ def tile_decoder_kernel(tc, table, gamma_t, beta_t, w, fine, gamma_f, beta_f, w_
                 fn[j][:], fine_sb[:, j * PIECE : (j + 1) * PIECE], scale_f[:], bias_f[:], op0=MULT, op1=ADD
             )
 
-        def open_bank(j, m):
-            bank[j, m] = banks.tile([P, PIECE], F32, name=f"bank{j}{m}", tag=f"bank{j % 3}{m}")
-            picked = tn[:].indirect(offsets[:, j * (PIECE // 16) : (j + 1) * (PIECE // 16)])
-            nc.tensor.matmul(bank[j, m][:], w_sb[:, m * P : (m + 1) * P], picked, start=True, stop=False)
+        def gathered(j, m, first, width, start, stop):
+            column = (j * PIECE + first) // 16
+            picked = tn[:].indirect(offsets[:, column : column + width // 16])
+            nc.tensor.matmul(
+                bank[j, m][:, first : first + width], w_sb[:, m * P : (m + 1) * P], picked, start=start, stop=stop
+            )
 
-        def close_bank(j, m):
-            for c in range(0, PIECE, SLICE):
-                nc.tensor.matmul(
-                    bank[j, m][:, c : c + SLICE],
-                    w_fine_sb[:, m * P : (m + 1) * P],
-                    fn[j][:, c : c + SLICE],
-                    start=False,
-                    stop=(c + SLICE == PIECE),
-                )
+        def plain(j, m, first, width, start, stop):
+            nc.tensor.matmul(
+                bank[j, m][:, first : first + width],
+                w_fine_sb[:, m * P : (m + 1) * P],
+                fn[j][:, first : first + width],
+                start=start,
+                stop=stop,
+            )
+
+        def store(j, m):
             staged = staging.tile([P, PIECE], F32, name="staged")
             if m == 0:
                 nc.scalar.copy(staged[:], bank[j, m][:])
@@ -115,11 +126,30 @@ def tile_decoder_kernel(tc, table, gamma_t, beta_t, w, fine, gamma_f, beta_f, w_
                 nc.vector.tensor_copy(staged[:], bank[j, m][:])
             nc.sync.dma_start(out[m * P : (m + 1) * P, j * PIECE : (j + 1) * PIECE], staged[:])
 
-        runs = [[(j, m) for j in range(0, 3) for m in range(M // P)], [(3, m) for m in range(M // P)]]
+        halves = range(M // P)
         with tc.psum_pool(name="banks", bufs=1) as banks:
             bank = {}
-            for corners in runs:
-                for j, m in corners:
-                    open_bank(j, m)
-                for j, m in corners:
-                    close_bank(j, m)
+            for j in (0, 1):
+                for m in halves:
+                    bank[j, m] = banks.tile([P, PIECE], F32, name=f"bank{j}{m}")
+                    gathered(j, m, 0, PIECE, start=True, stop=False)
+            for j in (0, 1):
+                for m in halves:
+                    for first in range(0, PIECE, SLICE):
+                        plain(j, m, first, SLICE, start=False, stop=(first + SLICE == PIECE))
+                    store(j, m)
+            for m in halves:
+                bank[2, m] = banks.tile([P, PIECE], F32, name=f"bank2{m}")
+                for first in range(0, PIECE, SLICE):
+                    plain(2, m, first, SLICE, start=(first == 0), stop=False)
+            for m in halves:
+                for first in range(0, PIECE, HALF):
+                    gathered(2, m, first, HALF, start=False, stop=(first + HALF == PIECE))
+            for m in halves:
+                bank[3, m] = banks.tile([P, PIECE], F32, name=f"bank3{m}", tag=f"bank0{m}")
+                gathered(3, m, 0, PIECE, start=True, stop=False)
+            for m in halves:
+                store(2, m)
+            for m in halves:
+                plain(3, m, 0, PIECE, start=False, stop=True)
+                store(3, m)

@@ -14,18 +14,19 @@ EPS = 1e-5
 PIECE = 512
 HALF = S // 2
 SLICE = 128
+SHORT = 256
 STATS = 6
 
 FLOPS = 2 * (P + P) * M * N
 
 
-def mean_and_rstd(nc, pool, rstd, stats, eps, minus_one, level):
+def mean_and_rstd(nc, pool, rstd, stats, eps, gamma, minus_one, level):
     mean_var = pool.tile([P, 2], F32, name="mean_var_" + level)
     nc.vector.bn_aggr(mean_var[:], stats)
     nc.scalar.activation(rstd[:], mean_var[:, 1:2], RSQRT, bias=eps[:], scale=1.0)
-    neg_mean = pool.tile([P, 1], F32, name="neg_mean_" + level)
-    nc.vector.tensor_scalar_mul(neg_mean[:], mean_var[:, 0:1], minus_one)
-    return neg_mean
+    neg_mean_gamma = pool.tile([P, 1], F32, name="neg_mean_gamma_" + level)
+    nc.vector.tensor_scalar(neg_mean_gamma[:], mean_var[:, 0:1], gamma, minus_one, op0=MULT, op1=MULT)
+    return neg_mean_gamma
 
 
 def tile_decoder_kernel(tc, table, gamma_t, beta_t, w, fine, gamma_f, beta_f, w_fine, offs, out):
@@ -33,7 +34,7 @@ def tile_decoder_kernel(tc, table, gamma_t, beta_t, w, fine, gamma_f, beta_f, w_
     with (
         tc.tile_pool(name="held", bufs=1) as held,
         tc.tile_pool(name="handover", bufs=1) as handover,
-        tc.tile_pool(name="staging", bufs=(N // PIECE) * (M // P)) as staging,
+        tc.tile_pool(name="staging", bufs=10) as staging,
     ):
         identity = held.tile([P, P], BF16, name="identity")
         nc.vector.memset(identity[:], 0.0)
@@ -75,11 +76,15 @@ def tile_decoder_kernel(tc, table, gamma_t, beta_t, w, fine, gamma_f, beta_f, w_
                     )
                 nc.vector.bn_stats(stats_t[:, h * STATS : (h + 1) * STATS], flipped[h][:])
             rstd_t = held.tile([P, 1], F32, name="rstd_t")
-            neg_mean_t = mean_and_rstd(nc, held, rstd_t, stats_t[:], eps, minus_one_t[:], "t")
+            neg_mean_gamma_t = mean_and_rstd(
+                nc, held, rstd_t, stats_t[:], eps, per_feature["gamma_t"][:], minus_one_t[:], "t"
+            )
             scale_t = held.tile([P, 1], F32, name="scale_t")
             nc.scalar.activation(scale_t[:], rstd_t[:], COPY, scale=per_feature["gamma_t"][:])
             bias_t = handover.tile([P, 1], F32, name="bias_t", tag="scalar_slot")
-            nc.scalar.activation(bias_t[:], neg_mean_t[:], IDENTITY, bias=per_feature["beta_t"][:], scale=scale_t[:])
+            nc.scalar.activation(
+                bias_t[:], rstd_t[:], IDENTITY, bias=per_feature["beta_t"][:], scale=neg_mean_gamma_t[:]
+            )
             for h in range(2):
                 nc.scalar.activation(
                     tn[:, h * HALF : (h + 1) * HALF], flipped[h][:], IDENTITY, bias=bias_t[:], scale=scale_t[:]
@@ -89,12 +94,12 @@ def tile_decoder_kernel(tc, table, gamma_t, beta_t, w, fine, gamma_f, beta_f, w_
         for j in range(N // PIECE):
             nc.vector.bn_stats(stats_f[:, j * STATS : (j + 1) * STATS], fine_sb[:, j * PIECE : (j + 1) * PIECE])
         rstd_f = handover.tile([P, 1], F32, name="rstd_f", tag="scalar_slot")
-        neg_mean_f = mean_and_rstd(nc, held, rstd_f, stats_f[:], eps, -1.0, "f")
+        neg_mean_gamma_f = mean_and_rstd(nc, held, rstd_f, stats_f[:], eps, per_feature["gamma_f"][:], -1.0, "f")
         scale_f = held.tile([P, 1], F32, name="scale_f")
         nc.vector.tensor_mul(scale_f[:], per_feature["gamma_f"][:], rstd_f[:])
         bias_f = held.tile([P, 1], F32, name="bias_f")
         nc.vector.scalar_tensor_tensor(
-            bias_f[:], neg_mean_f[:], scale_f[:], per_feature["beta_f"][:], op0=MULT, op1=ADD
+            bias_f[:], neg_mean_gamma_f[:], rstd_f[:], per_feature["beta_f"][:], op0=MULT, op1=ADD
         )
         fn = [held.tile([P, PIECE], BF16, name=f"fn{j}") for j in range(N // PIECE)]
         for j in range(N // PIECE):
@@ -102,29 +107,24 @@ def tile_decoder_kernel(tc, table, gamma_t, beta_t, w, fine, gamma_f, beta_f, w_
                 fn[j][:], fine_sb[:, j * PIECE : (j + 1) * PIECE], scale_f[:], bias_f[:], op0=MULT, op1=ADD
             )
 
-        def gathered(j, m, first, width, start, stop):
-            column = (j * PIECE + first) // 16
-            picked = tn[:].indirect(offsets[:, column : column + width // 16])
-            nc.tensor.matmul(
-                bank[j, m][:, first : first + width], w_sb[:, m * P : (m + 1) * P], picked, start=start, stop=stop
-            )
+        def gathered(dest, m, column, start, stop):
+            width = dest.shape[1]
+            picked = tn[:].indirect(offsets[:, column // 16 : (column + width) // 16])
+            nc.tensor.matmul(dest, w_sb[:, m * P : (m + 1) * P], picked, start=start, stop=stop)
 
-        def plain(j, m, first, width, start, stop):
-            nc.tensor.matmul(
-                bank[j, m][:, first : first + width],
-                w_fine_sb[:, m * P : (m + 1) * P],
-                fn[j][:, first : first + width],
-                start=start,
-                stop=stop,
-            )
+        def plain(dest, m, column, start, stop):
+            j, first = divmod(column, PIECE)
+            moving = fn[j][:, first : first + dest.shape[1]]
+            nc.tensor.matmul(dest, w_fine_sb[:, m * P : (m + 1) * P], moving, start=start, stop=stop)
 
-        def store(j, m):
-            staged = staging.tile([P, PIECE], F32, name="staged")
+        def store(source, m, column):
+            width = source.shape[1]
+            staged = staging.tile([P, width], F32, name="staged")
             if m == 0:
-                nc.scalar.copy(staged[:], bank[j, m][:])
+                nc.scalar.copy(staged[:], source)
             else:
-                nc.vector.tensor_copy(staged[:], bank[j, m][:])
-            nc.sync.dma_start(out[m * P : (m + 1) * P, j * PIECE : (j + 1) * PIECE], staged[:])
+                nc.vector.tensor_copy(staged[:], source)
+            nc.sync.dma_start(out[m * P : (m + 1) * P, column : column + width], staged[:])
 
         halves = range(M // P)
         with tc.psum_pool(name="banks", bufs=1) as banks:
@@ -132,24 +132,28 @@ def tile_decoder_kernel(tc, table, gamma_t, beta_t, w, fine, gamma_f, beta_f, w_
             for j in (0, 1):
                 for m in halves:
                     bank[j, m] = banks.tile([P, PIECE], F32, name=f"bank{j}{m}")
-                    gathered(j, m, 0, PIECE, start=True, stop=False)
+                    gathered(bank[j, m][:], m, j * PIECE, start=True, stop=False)
             for j in (0, 1):
                 for m in halves:
                     for first in range(0, PIECE, SLICE):
-                        plain(j, m, first, SLICE, start=False, stop=(first + SLICE == PIECE))
-                    store(j, m)
+                        last = first + SLICE == PIECE
+                        plain(bank[j, m][:, first : first + SLICE], m, j * PIECE + first, start=False, stop=last)
+                    store(bank[j, m][:], m, j * PIECE)
             for m in halves:
                 bank[2, m] = banks.tile([P, PIECE], F32, name=f"bank2{m}")
                 for first in range(0, PIECE, SLICE):
-                    plain(2, m, first, SLICE, start=(first == 0), stop=False)
+                    plain(bank[2, m][:, first : first + SLICE], m, 2 * PIECE + first, start=(first == 0), stop=False)
             for m in halves:
-                for first in range(0, PIECE, HALF):
-                    gathered(2, m, first, HALF, start=False, stop=(first + HALF == PIECE))
+                for first in range(0, PIECE, SHORT):
+                    last = first + SHORT == PIECE
+                    gathered(bank[2, m][:, first : first + SHORT], m, 2 * PIECE + first, start=False, stop=last)
+            for h in range(PIECE // SHORT):
+                for m in halves:
+                    bank[3, h, m] = banks.tile([P, SHORT], F32, name=f"bank3{h}{m}", tag=f"bank{h}{m}")
+                    gathered(bank[3, h, m][:], m, 3 * PIECE + h * SHORT, start=True, stop=False)
             for m in halves:
-                bank[3, m] = banks.tile([P, PIECE], F32, name=f"bank3{m}", tag=f"bank0{m}")
-                gathered(3, m, 0, PIECE, start=True, stop=False)
-            for m in halves:
-                store(2, m)
-            for m in halves:
-                plain(3, m, 0, PIECE, start=False, stop=True)
-                store(3, m)
+                store(bank[2, m][:], m, 2 * PIECE)
+            for h in range(PIECE // SHORT):
+                for m in halves:
+                    plain(bank[3, h, m][:], m, 3 * PIECE + h * SHORT, start=False, stop=True)
+                    store(bank[3, h, m][:], m, 3 * PIECE + h * SHORT)

@@ -13,6 +13,7 @@ N = 2048
 EPS = 1e-5
 PIECE = 512
 HALF = S // 2
+PAIR = HALF // P
 SLICE = 128
 SHORT = 256
 STATS = 6
@@ -34,7 +35,7 @@ def tile_decoder_kernel(tc, table, gamma_t, beta_t, w, fine, gamma_f, beta_f, w_
     with (
         tc.tile_pool(name="held", bufs=1) as held,
         tc.tile_pool(name="handover", bufs=1) as handover,
-        tc.tile_pool(name="staging", bufs=10) as staging,
+        tc.tile_pool(name="staging", bufs=(N // PIECE) * (M // P)) as staging,
     ):
         identity = held.tile([P, P], BF16, name="identity")
         nc.vector.memset(identity[:], 0.0)
@@ -44,8 +45,8 @@ def tile_decoder_kernel(tc, table, gamma_t, beta_t, w, fine, gamma_f, beta_f, w_
         minus_one_t = handover.tile([P, 1], F32, name="minus_one_t", tag="slot")
         nc.vector.memset(minus_one_t[:], -1.0)
 
-        rows = held.tile([P, S // P, P], BF16, name="rows")
-        nc.sync.dma_start(rows[:], table.rearrange("(r p) d -> p r d", p=P))
+        rows = held.tile([P, 2, PAIR, P], BF16, name="rows")
+        nc.sync.dma_start(rows[:], table.rearrange("(h p r) d -> p h r d", h=2, r=PAIR))
         fine_sb = held.tile([P, N], F32, name="fine_sb")
         for first, last in ((0, PIECE), (PIECE, 2 * PIECE), (2 * PIECE, N)):
             nc.sync.dma_start(fine_sb[:, first:last], fine[:, first:last])
@@ -70,10 +71,8 @@ def tile_decoder_kernel(tc, table, gamma_t, beta_t, w, fine, gamma_f, beta_f, w_
             flipped = [flip.tile([P, HALF], BF16, name=f"flipped{h}") for h in range(2)]
             stats_t = held.tile([P, 2 * STATS], F32, name="stats_t")
             for h in range(2):
-                for r in range(HALF // P):
-                    nc.tensor.transpose(
-                        flipped[h][:, r * P : (r + 1) * P], rows[:, h * (HALF // P) + r, :], identity[:]
-                    )
+                for r in range(PAIR):
+                    nc.tensor.transpose(flipped[h][:, r * P : (r + 1) * P], rows[:, h, r, :], identity[:])
                 nc.vector.bn_stats(stats_t[:, h * STATS : (h + 1) * STATS], flipped[h][:])
             rstd_t = held.tile([P, 1], F32, name="rstd_t")
             neg_mean_gamma_t = mean_and_rstd(
@@ -87,7 +86,11 @@ def tile_decoder_kernel(tc, table, gamma_t, beta_t, w, fine, gamma_f, beta_f, w_
             )
             for h in range(2):
                 nc.scalar.activation(
-                    tn[:, h * HALF : (h + 1) * HALF], flipped[h][:], IDENTITY, bias=bias_t[:], scale=scale_t[:]
+                    tn[:, h * HALF : (h + 1) * HALF].rearrange("d (p r) -> d p r", r=PAIR),
+                    flipped[h][:].rearrange("d (r p) -> d p r", r=PAIR),
+                    IDENTITY,
+                    bias=bias_t[:],
+                    scale=scale_t[:],
                 )
 
         stats_f = handover.tile([P, (N // PIECE) * STATS], F32, name="stats_f", tag="slot")
@@ -117,14 +120,13 @@ def tile_decoder_kernel(tc, table, gamma_t, beta_t, w, fine, gamma_f, beta_f, w_
             moving = fn[j][:, first : first + dest.shape[1]]
             nc.tensor.matmul(dest, w_fine_sb[:, m * P : (m + 1) * P], moving, start=start, stop=stop)
 
-        def store(source, m, column):
-            width = source.shape[1]
-            staged = staging.tile([P, width], F32, name="staged")
+        def store(j, m):
+            staged = staging.tile([P, PIECE], F32, name="staged")
             if m == 0:
-                nc.scalar.copy(staged[:], source)
+                nc.scalar.copy(staged[:], bank[j, m][:])
             else:
-                nc.vector.tensor_copy(staged[:], source)
-            nc.sync.dma_start(out[m * P : (m + 1) * P, column : column + width], staged[:])
+                nc.vector.tensor_copy(staged[:], bank[j, m][:])
+            nc.sync.dma_start(out[m * P : (m + 1) * P, j * PIECE : (j + 1) * PIECE], staged[:])
 
         halves = range(M // P)
         with tc.psum_pool(name="banks", bufs=1) as banks:
@@ -138,7 +140,7 @@ def tile_decoder_kernel(tc, table, gamma_t, beta_t, w, fine, gamma_f, beta_f, w_
                     for first in range(0, PIECE, SLICE):
                         last = first + SLICE == PIECE
                         plain(bank[j, m][:, first : first + SLICE], m, j * PIECE + first, start=False, stop=last)
-                    store(bank[j, m][:], m, j * PIECE)
+                    store(j, m)
             for m in halves:
                 bank[2, m] = banks.tile([P, PIECE], F32, name=f"bank2{m}")
                 for first in range(0, PIECE, SLICE):
@@ -147,13 +149,11 @@ def tile_decoder_kernel(tc, table, gamma_t, beta_t, w, fine, gamma_f, beta_f, w_
                 for first in range(0, PIECE, SHORT):
                     last = first + SHORT == PIECE
                     gathered(bank[2, m][:, first : first + SHORT], m, 2 * PIECE + first, start=False, stop=last)
-            for h in range(PIECE // SHORT):
-                for m in halves:
-                    bank[3, h, m] = banks.tile([P, SHORT], F32, name=f"bank3{h}{m}", tag=f"bank{h}{m}")
-                    gathered(bank[3, h, m][:], m, 3 * PIECE + h * SHORT, start=True, stop=False)
             for m in halves:
-                store(bank[2, m][:], m, 2 * PIECE)
-            for h in range(PIECE // SHORT):
-                for m in halves:
-                    plain(bank[3, h, m][:], m, 3 * PIECE + h * SHORT, start=False, stop=True)
-                    store(bank[3, h, m][:], m, 3 * PIECE + h * SHORT)
+                bank[3, m] = banks.tile([P, PIECE], F32, name=f"bank3{m}", tag=f"bank0{m}")
+                gathered(bank[3, m][:], m, 3 * PIECE, start=True, stop=False)
+            for m in halves:
+                store(2, m)
+            for m in halves:
+                plain(bank[3, m][:], m, 3 * PIECE, start=False, stop=True)
+                store(3, m)

@@ -48,23 +48,18 @@ def tile_decoder_kernel(tc, table, gamma_t, beta_t, w, fine, gamma_f, beta_f, w_
         rows = held.tile([P, 2, PAIR, P], BF16, name="rows")
         nc.sync.dma_start(rows[:], table.rearrange("(h p r) d -> p h r d", h=2, r=PAIR))
         fine_sb = held.tile([P, N], F32, name="fine_sb")
-        for first, last in ((0, PIECE), (PIECE, 2 * PIECE), (2 * PIECE, N)):
+        for first, last in ((0, N // 2), (N // 2, N)):
             nc.sync.dma_start(fine_sb[:, first:last], fine[:, first:last])
         offsets = held.tile([P, N // 16], U16, name="offsets")
         nc.sync.dma_start(offsets[:], offs)
         w_sb = held.tile([P, M], BF16, name="w_sb")
         nc.sync.dma_start(w_sb[:], w)
         per_feature = {}
-        for label, vector, queue in (
-            ("gamma_t", gamma_t, nc.scalar),
-            ("beta_t", beta_t, nc.scalar),
-            ("gamma_f", gamma_f, nc.gpsimd),
-            ("beta_f", beta_f, nc.gpsimd),
-        ):
+        for label, vector in (("gamma_t", gamma_t), ("beta_t", beta_t), ("gamma_f", gamma_f), ("beta_f", beta_f)):
             per_feature[label] = held.tile([P, 1], F32, name=label + "_sb")
-            queue.dma_start(per_feature[label][:], vector)
+            nc.scalar.dma_start(per_feature[label][:], vector)
         w_fine_sb = held.tile([P, M], BF16, name="w_fine_sb")
-        nc.gpsimd.dma_start(w_fine_sb[:], w_fine)
+        nc.sync.dma_start(w_fine_sb[:], w_fine)
 
         tn = held.tile([P, S], BF16, name="tn")
         with tc.psum_pool(name="flip", bufs=1) as flip:

@@ -47,13 +47,13 @@ def tile_decoder_kernel(tc, table, gamma_t, beta_t, w, fine, gamma_f, beta_f, w_
 
         rows = held.tile([P, 2, PAIR, P], BF16, name="rows")
         nc.sync.dma_start(rows[:], table.rearrange("(h p r) d -> p h r d", h=2, r=PAIR))
-        fine_sb = held.tile([P, N], F32, name="fine_sb")
-        for first, last in ((0, N // 2), (N // 2, N)):
-            nc.sync.dma_start(fine_sb[:, first:last], fine[:, first:last])
         offsets = held.tile([P, N // 16], U16, name="offsets")
         nc.sync.dma_start(offsets[:], offs)
         w_sb = held.tile([P, M], BF16, name="w_sb")
         nc.sync.dma_start(w_sb[:], w)
+        fine_sb = held.tile([P, N], F32, name="fine_sb")
+        for first, last in ((0, N // 2), (N // 2, N)):
+            nc.sync.dma_start(fine_sb[:, first:last], fine[:, first:last])
         per_feature = {}
         for label, vector in (("gamma_t", gamma_t), ("beta_t", beta_t), ("gamma_f", gamma_f), ("beta_f", beta_f)):
             per_feature[label] = held.tile([P, 1], F32, name=label + "_sb")

@@ -47,13 +47,13 @@ def tile_decoder_kernel(tc, table, gamma_t, beta_t, w, fine, gamma_f, beta_f, w_
 
         rows = held.tile([P, 2, PAIR, P], BF16, name="rows")
         nc.sync.dma_start(rows[:], table.rearrange("(h p r) d -> p h r d", h=2, r=PAIR))
+        fine_sb = held.tile([P, N], F32, name="fine_sb")
+        for first, last in ((0, N // 2), (N // 2, N)):
+            nc.sync.dma_start(fine_sb[:, first:last], fine[:, first:last])
         offsets = held.tile([P, N // 16], U16, name="offsets")
         nc.sync.dma_start(offsets[:], offs)
         w_sb = held.tile([P, M], BF16, name="w_sb")
         nc.sync.dma_start(w_sb[:], w)
-        fine_sb = held.tile([P, N], F32, name="fine_sb")
-        for first, last in ((0, N // 2), (N // 2, N)):
-            nc.sync.dma_start(fine_sb[:, first:last], fine[:, first:last])
         per_feature = {}
         for label, vector in (("gamma_t", gamma_t), ("beta_t", beta_t), ("gamma_f", gamma_f), ("beta_f", beta_f)):
             per_feature[label] = held.tile([P, 1], F32, name=label + "_sb")
@@ -125,10 +125,9 @@ def tile_decoder_kernel(tc, table, gamma_t, beta_t, w, fine, gamma_f, beta_f, w_
 
         halves = range(M // P)
         with tc.psum_pool(name="banks", bufs=1) as banks:
-            bank = {}
+            bank = {(j, m): banks.tile([P, PIECE], F32, name=f"bank{j}{m}") for j in range(N // PIECE) for m in halves}
             for j in (0, 1):
                 for m in halves:
-                    bank[j, m] = banks.tile([P, PIECE], F32, name=f"bank{j}{m}")
                     gathered(bank[j, m][:], m, j * PIECE, start=True, stop=False)
             for j in (0, 1):
                 for m in halves:
@@ -136,19 +135,13 @@ def tile_decoder_kernel(tc, table, gamma_t, beta_t, w, fine, gamma_f, beta_f, w_
                         last = first + SLICE == PIECE
                         plain(bank[j, m][:, first : first + SLICE], m, j * PIECE + first, start=False, stop=last)
                     store(j, m)
-            for m in halves:
-                bank[2, m] = banks.tile([P, PIECE], F32, name=f"bank2{m}")
-                for first in range(0, PIECE, SLICE):
-                    plain(bank[2, m][:, first : first + SLICE], m, 2 * PIECE + first, start=(first == 0), stop=False)
-            for m in halves:
-                for first in range(0, PIECE, SHORT):
-                    last = first + SHORT == PIECE
-                    gathered(bank[2, m][:, first : first + SHORT], m, 2 * PIECE + first, start=False, stop=last)
-            for m in halves:
-                bank[3, m] = banks.tile([P, PIECE], F32, name=f"bank3{m}", tag=f"bank0{m}")
-                gathered(bank[3, m][:], m, 3 * PIECE, start=True, stop=False)
-            for m in halves:
-                store(2, m)
-            for m in halves:
-                plain(bank[3, m][:], m, 3 * PIECE, start=False, stop=True)
-                store(3, m)
+            for j in (2, 3):
+                for m in halves:
+                    for first in range(0, PIECE, SHORT):
+                        plain(bank[j, m][:, first : first + SHORT], m, j * PIECE + first, start=(first == 0), stop=False)
+            for j in (2, 3):
+                for m in halves:
+                    for first in range(0, PIECE, SHORT):
+                        last = first + SHORT == PIECE
+                        gathered(bank[j, m][:, first : first + SHORT], m, j * PIECE + first, start=False, stop=last)
+                    store(j, m)

@@ -21,12 +21,12 @@ STATS = 6
 FLOPS = 2 * (P + P) * M * N
 
 
-def mean_and_rstd(nc, pool, rstd, stats, eps, gamma, minus_one, level):
+def mean_and_rstd(nc, pool, rstd, stats, eps, gamma, helper, level):
     mean_var = pool.tile([P, 2], F32, name="mean_var_" + level)
     nc.vector.bn_aggr(mean_var[:], stats)
     nc.scalar.activation(rstd[:], mean_var[:, 1:2], RSQRT, bias=eps[:], scale=1.0)
     neg_mean_gamma = pool.tile([P, 1], F32, name="neg_mean_gamma_" + level)
-    nc.vector.tensor_scalar(neg_mean_gamma[:], mean_var[:, 0:1], gamma, minus_one, op0=MULT, op1=MULT)
+    helper.tensor_scalar(neg_mean_gamma[:], mean_var[:, 0:1], gamma, -1.0, op0=MULT, op1=MULT)
     return neg_mean_gamma
 
 
@@ -42,8 +42,6 @@ def tile_decoder_kernel(tc, table, gamma_t, beta_t, w, fine, gamma_f, beta_f, w_
         make_identity(nc, identity[:], nomemset=True)
         eps = held.tile([P, 1], F32, name="eps")
         nc.vector.memset(eps[:], EPS)
-        minus_one_t = handover.tile([P, 1], F32, name="minus_one_t", tag="slot")
-        nc.vector.memset(minus_one_t[:], -1.0)
 
         rows = held.tile([P, 2, PAIR, P], BF16, name="rows")
         nc.sync.dma_start(rows[:], table.rearrange("(h p r) d -> p h r d", h=2, r=PAIR))
@@ -64,14 +62,14 @@ def tile_decoder_kernel(tc, table, gamma_t, beta_t, w, fine, gamma_f, beta_f, w_
         tn = held.tile([P, S], BF16, name="tn")
         with tc.psum_pool(name="flip", bufs=1) as flip:
             flipped = [flip.tile([P, HALF], BF16, name=f"flipped{h}") for h in range(2)]
-            stats_t = held.tile([P, 2 * STATS], F32, name="stats_t")
+            stats_t = handover.tile([P, 2 * STATS], F32, name="stats_t", tag="slot")
             for h in range(2):
                 for r in range(PAIR):
                     nc.tensor.transpose(flipped[h][:, r * P : (r + 1) * P], rows[:, h, r, :], identity[:])
                 nc.vector.bn_stats(stats_t[:, h * STATS : (h + 1) * STATS], flipped[h][:])
             rstd_t = held.tile([P, 1], F32, name="rstd_t")
             neg_mean_gamma_t = mean_and_rstd(
-                nc, held, rstd_t, stats_t[:], eps, per_feature["gamma_t"][:], minus_one_t[:], "t"
+                nc, held, rstd_t, stats_t[:], eps, per_feature["gamma_t"][:], nc.gpsimd, "t"
             )
             scale_t = held.tile([P, 1], F32, name="scale_t")
             nc.scalar.activation(scale_t[:], rstd_t[:], COPY, scale=per_feature["gamma_t"][:])
@@ -92,7 +90,7 @@ def tile_decoder_kernel(tc, table, gamma_t, beta_t, w, fine, gamma_f, beta_f, w_
         for j in range(N // PIECE):
             nc.vector.bn_stats(stats_f[:, j * STATS : (j + 1) * STATS], fine_sb[:, j * PIECE : (j + 1) * PIECE])
         rstd_f = handover.tile([P, 1], F32, name="rstd_f", tag="scalar_slot")
-        neg_mean_gamma_f = mean_and_rstd(nc, held, rstd_f, stats_f[:], eps, per_feature["gamma_f"][:], -1.0, "f")
+        neg_mean_gamma_f = mean_and_rstd(nc, held, rstd_f, stats_f[:], eps, per_feature["gamma_f"][:], nc.vector, "f")
         scale_f = held.tile([P, 1], F32, name="scale_f")
         nc.vector.tensor_mul(scale_f[:], per_feature["gamma_f"][:], rstd_f[:])
         bias_f = held.tile([P, 1], F32, name="bias_f")

@@ -16,6 +16,7 @@ HALF = S // 2
 PAIR = HALF // P
 SLICE = 128
 SHORT = 256
+OPENED = 4
 STATS = 6
 
 FLOPS = 2 * (P + P) * M * N
@@ -46,7 +47,7 @@ def tile_decoder_kernel(tc, table, gamma_t, beta_t, w, fine, gamma_f, beta_f, w_
         rows = held.tile([P, 2, PAIR, P], BF16, name="rows")
         nc.sync.dma_start(rows[:], table.rearrange("(h p r) d -> p h r d", h=2, r=PAIR))
         fine_sb = held.tile([P, N], F32, name="fine_sb")
-        for first, last in ((0, N // 2), (N // 2, N)):
+        for first, last in ((0, N // 2), (N // 2, N - PIECE), (N - PIECE, N)):
             nc.sync.dma_start(fine_sb[:, first:last], fine[:, first:last])
         offsets = held.tile([P, N // 16], U16, name="offsets")
         nc.sync.dma_start(offsets[:], offs)
@@ -121,25 +122,21 @@ def tile_decoder_kernel(tc, table, gamma_t, beta_t, w, fine, gamma_f, beta_f, w_
                 nc.vector.tensor_copy(staged[:], bank[j, m][:])
             nc.sync.dma_start(out[m * P : (m + 1) * P, j * PIECE : (j + 1) * PIECE], staged[:])
 
-        halves = range(M // P)
         with tc.psum_pool(name="banks", bufs=1) as banks:
-            bank = {(j, m): banks.tile([P, PIECE], F32, name=f"bank{j}{m}") for j in range(N // PIECE) for m in halves}
-            for j in (0, 1):
-                for m in halves:
-                    gathered(bank[j, m][:], m, j * PIECE, start=True, stop=False)
-            for j in (0, 1):
-                for m in halves:
-                    for first in range(0, PIECE, SLICE):
-                        last = first + SLICE == PIECE
-                        plain(bank[j, m][:, first : first + SLICE], m, j * PIECE + first, start=False, stop=last)
-                    store(j, m)
-            for j in (2, 3):
-                for m in halves:
-                    for first in range(0, PIECE, SHORT):
-                        plain(bank[j, m][:, first : first + SHORT], m, j * PIECE + first, start=(first == 0), stop=False)
-            for j in (2, 3):
-                for m in halves:
-                    for first in range(0, PIECE, SHORT):
-                        last = first + SHORT == PIECE
-                        gathered(bank[j, m][:, first : first + SHORT], m, j * PIECE + first, start=False, stop=last)
-                    store(j, m)
+            order = [(j, m) for j in range(N // PIECE) for m in range(M // P)]
+            bank = {(j, m): banks.tile([P, PIECE], F32, name=f"bank{j}{m}") for j, m in order}
+            for j, m in order[:OPENED]:
+                gathered(bank[j, m][:], m, j * PIECE, start=True, stop=False)
+            for j, m in order[:OPENED]:
+                for first in range(0, PIECE, SLICE):
+                    last = first + SLICE == PIECE
+                    plain(bank[j, m][:, first : first + SLICE], m, j * PIECE + first, start=False, stop=last)
+                store(j, m)
+            for j, m in order[OPENED:]:
+                for first in range(0, PIECE, SHORT):
+                    plain(bank[j, m][:, first : first + SHORT], m, j * PIECE + first, start=(first == 0), stop=False)
+            for j, m in order[OPENED:]:
+                for first in range(0, PIECE, SHORT):
+                    last = first + SHORT == PIECE
+                    gathered(bank[j, m][:, first : first + SHORT], m, j * PIECE + first, start=False, stop=last)
+                store(j, m)

@@ -17,6 +17,7 @@ PAIR = HALF // P
 SLICE = 128
 SHORT = 256
 OPENED = 4
+HEAD = 256
 STATS = 6
 
 FLOPS = 2 * (P + P) * M * N
@@ -47,7 +48,7 @@ def tile_decoder_kernel(tc, table, gamma_t, beta_t, w, fine, gamma_f, beta_f, w_
         rows = held.tile([P, 2, PAIR, P], BF16, name="rows")
         nc.sync.dma_start(rows[:], table.rearrange("(h p r) d -> p h r d", h=2, r=PAIR))
         fine_sb = held.tile([P, N], F32, name="fine_sb")
-        for first, last in ((0, N // 2), (N // 2, N - PIECE), (N - PIECE, N)):
+        for first, last in ((0, HEAD), (HEAD, HEAD + 2 * PIECE), (HEAD + 2 * PIECE, N)):
             nc.sync.dma_start(fine_sb[:, first:last], fine[:, first:last])
         offsets = held.tile([P, N // 16], U16, name="offsets")
         nc.sync.dma_start(offsets[:], offs)
@@ -59,6 +60,9 @@ def tile_decoder_kernel(tc, table, gamma_t, beta_t, w, fine, gamma_f, beta_f, w_
             nc.scalar.dma_start(per_feature[label][:], vector)
         w_fine_sb = held.tile([P, M], BF16, name="w_fine_sb")
         nc.sync.dma_start(w_fine_sb[:], w_fine)
+
+        stats_head = held.tile([P, STATS], F32, name="stats_head")
+        nc.vector.bn_stats(stats_head[:], fine_sb[:, 0:HEAD])
 
         tn = held.tile([P, S], BF16, name="tn")
         with tc.psum_pool(name="flip", bufs=1) as flip:
@@ -87,9 +91,11 @@ def tile_decoder_kernel(tc, table, gamma_t, beta_t, w, fine, gamma_f, beta_f, w_
                     scale=scale_t[:],
                 )
 
-        stats_f = handover.tile([P, (N // PIECE) * STATS], F32, name="stats_f", tag="slot")
-        for j in range(N // PIECE):
-            nc.vector.bn_stats(stats_f[:, j * STATS : (j + 1) * STATS], fine_sb[:, j * PIECE : (j + 1) * PIECE])
+        edges = [0] + list(range(HEAD, N, PIECE)) + [N]
+        stats_f = handover.tile([P, (len(edges) - 1) * STATS], F32, name="stats_f", tag="slot")
+        nc.vector.tensor_copy(stats_f[:, 0:STATS], stats_head[:])
+        for k in range(1, len(edges) - 1):
+            nc.vector.bn_stats(stats_f[:, k * STATS : (k + 1) * STATS], fine_sb[:, edges[k] : edges[k + 1]])
         rstd_f = handover.tile([P, 1], F32, name="rstd_f", tag="scalar_slot")
         neg_mean_gamma_f = mean_and_rstd(nc, held, rstd_f, stats_f[:], eps, per_feature["gamma_f"][:], nc.vector, "f")
         scale_f = held.tile([P, 1], F32, name="scale_f")

import concourse.mybir as mybir
from concourse.masks import make_identity

BF16, F32, U16 = mybir.dt.bfloat16, mybir.dt.float32, mybir.dt.uint16
MULT, ADD = mybir.AluOpType.mult, mybir.AluOpType.add
RSQRT = mybir.ActivationFunctionType.Abs_reciprocal_sqrt
IDENTITY, COPY = mybir.ActivationFunctionType.Identity, mybir.ActivationFunctionType.Copy

P = 128
S = 512
M = 256
N = 2048
EPS = 1e-5
PIECE = 512
HALF = S // 2
PAIR = HALF // P
SLICE = 128
SHORT = 256
OPENED = 4
HEAD = 256
STATS = 6

FLOPS = 2 * (P + P) * M * N


def mean_and_rstd(nc, pool, rstd, stats, eps, gamma, helper, level):
    mean_var = pool.tile([P, 2], F32, name="mean_var_" + level)
    nc.vector.bn_aggr(mean_var[:], stats)
    nc.scalar.activation(rstd[:], mean_var[:, 1:2], RSQRT, bias=eps[:], scale=1.0)
    neg_mean_gamma = pool.tile([P, 1], F32, name="neg_mean_gamma_" + level)
    helper.tensor_scalar(neg_mean_gamma[:], mean_var[:, 0:1], gamma, -1.0, op0=MULT, op1=MULT)
    return neg_mean_gamma


def tile_decoder_kernel(tc, table, gamma_t, beta_t, w, fine, gamma_f, beta_f, w_fine, offs, out):
    nc = tc.nc
    with (
        tc.tile_pool(name="held", bufs=1) as held,
        tc.tile_pool(name="handover", bufs=1) as handover,
        tc.tile_pool(name="staging", bufs=(N // PIECE) * (M // P)) as staging,
    ):
        identity = held.tile([P, P], BF16, name="identity")
        nc.vector.memset(identity[:], 0.0)
        make_identity(nc, identity[:], nomemset=True)
        eps = held.tile([P, 1], F32, name="eps")
        nc.vector.memset(eps[:], EPS)

        rows = held.tile([P, 2, PAIR, P], BF16, name="rows")
        nc.sync.dma_start(rows[:], table.rearrange("(h p r) d -> p h r d", h=2, r=PAIR))
        fine_sb = held.tile([P, N], F32, name="fine_sb")
        for first, last in ((0, HEAD), (HEAD, HEAD + 2 * PIECE), (HEAD + 2 * PIECE, N)):
            nc.sync.dma_start(fine_sb[:, first:last], fine[:, first:last])
        offsets = held.tile([P, N // 16], U16, name="offsets")
        nc.sync.dma_start(offsets[:], offs)
        w_sb = held.tile([P, M], BF16, name="w_sb")
        nc.sync.dma_start(w_sb[:], w)
        per_feature = {}
        for label, vector in (("gamma_t", gamma_t), ("beta_t", beta_t), ("gamma_f", gamma_f), ("beta_f", beta_f)):
            per_feature[label] = held.tile([P, 1], F32, name=label + "_sb")
            nc.scalar.dma_start(per_feature[label][:], vector)
        w_fine_sb = held.tile([P, M], BF16, name="w_fine_sb")
        nc.sync.dma_start(w_fine_sb[:], w_fine)

        stats_head = held.tile([P, STATS], F32, name="stats_head")
        nc.vector.bn_stats(stats_head[:], fine_sb[:, 0:HEAD])

        tn = held.tile([P, S], BF16, name="tn")
        with tc.psum_pool(name="flip", bufs=1) as flip:
            flipped = [flip.tile([P, HALF], BF16, name=f"flipped{h}") for h in range(2)]
            stats_t = handover.tile([P, 2 * STATS], F32, name="stats_t", tag="slot")
            for h in range(2):
                for r in range(PAIR):
                    nc.tensor.transpose(flipped[h][:, r * P : (r + 1) * P], rows[:, h, r, :], identity[:])
                nc.vector.bn_stats(stats_t[:, h * STATS : (h + 1) * STATS], flipped[h][:])
            rstd_t = held.tile([P, 1], F32, name="rstd_t")
            neg_mean_gamma_t = mean_and_rstd(
                nc, held, rstd_t, stats_t[:], eps, per_feature["gamma_t"][:], nc.gpsimd, "t"
            )
            scale_t = held.tile([P, 1], F32, name="scale_t")
            nc.scalar.activation(scale_t[:], rstd_t[:], COPY, scale=per_feature["gamma_t"][:])
            bias_t = handover.tile([P, 1], F32, name="bias_t", tag="scalar_slot")
            nc.scalar.activation(
                bias_t[:], rstd_t[:], IDENTITY, bias=per_feature["beta_t"][:], scale=neg_mean_gamma_t[:]
            )
            for h in range(2):
                nc.scalar.activation(
                    tn[:, h * HALF : (h + 1) * HALF].rearrange("d (p r) -> d p r", r=PAIR),
                    flipped[h][:].rearrange("d (r p) -> d p r", r=PAIR),
                    IDENTITY,
                    bias=bias_t[:],
                    scale=scale_t[:],
                )

        edges = [0] + list(range(HEAD, N, PIECE)) + [N]
        stats_f = handover.tile([P, (len(edges) - 1) * STATS], F32, name="stats_f", tag="slot")
        nc.vector.tensor_copy(stats_f[:, 0:STATS], stats_head[:])
        for k in range(1, len(edges) - 1):
            nc.vector.bn_stats(stats_f[:, k * STATS : (k + 1) * STATS], fine_sb[:, edges[k] : edges[k + 1]])
        rstd_f = handover.tile([P, 1], F32, name="rstd_f", tag="scalar_slot")
        neg_mean_gamma_f = mean_and_rstd(nc, held, rstd_f, stats_f[:], eps, per_feature["gamma_f"][:], nc.vector, "f")
        scale_f = held.tile([P, 1], F32, name="scale_f")
        nc.vector.tensor_mul(scale_f[:], per_feature["gamma_f"][:], rstd_f[:])
        bias_f = held.tile([P, 1], F32, name="bias_f")
        nc.vector.scalar_tensor_tensor(
            bias_f[:], neg_mean_gamma_f[:], rstd_f[:], per_feature["beta_f"][:], op0=MULT, op1=ADD
        )
        fn = [held.tile([P, PIECE], BF16, name=f"fn{j}") for j in range(N // PIECE)]
        for j in range(N // PIECE):
            nc.vector.tensor_scalar(
                fn[j][:], fine_sb[:, j * PIECE : (j + 1) * PIECE], scale_f[:], bias_f[:], op0=MULT, op1=ADD
            )

        def gathered(dest, m, column, start, stop):
            width = dest.shape[1]
            picked = tn[:].indirect(offsets[:, column // 16 : (column + width) // 16])
            nc.tensor.matmul(dest, w_sb[:, m * P : (m + 1) * P], picked, start=start, stop=stop)

        def plain(dest, m, column, start, stop):
            j, first = divmod(column, PIECE)
            moving = fn[j][:, first : first + dest.shape[1]]
            nc.tensor.matmul(dest, w_fine_sb[:, m * P : (m + 1) * P], moving, start=start, stop=stop)

        def store(j, m):
            staged = staging.tile([P, PIECE], F32, name="staged")
            if m == 0:
                nc.scalar.copy(staged[:], bank[j, m][:])
            else:
                nc.vector.tensor_copy(staged[:], bank[j, m][:])
            nc.sync.dma_start(out[m * P : (m + 1) * P, j * PIECE : (j + 1) * PIECE], staged[:])

        with tc.psum_pool(name="banks", bufs=1) as banks:
            order = [(j, m) for j in range(N // PIECE) for m in range(M // P)]
            bank = {(j, m): banks.tile([P, PIECE], F32, name=f"bank{j}{m}") for j, m in order}
            for j, m in order[:OPENED]:
                gathered(bank[j, m][:], m, j * PIECE, start=True, stop=False)
            for j, m in order[:OPENED]:
                for first in range(0, PIECE, SLICE):
                    last = first + SLICE == PIECE
                    plain(bank[j, m][:, first : first + SLICE], m, j * PIECE + first, start=False, stop=last)
                store(j, m)
            for j, m in order[OPENED:]:
                for first in range(0, PIECE, SHORT):
                    plain(bank[j, m][:, first : first + SHORT], m, j * PIECE + first, start=(first == 0), stop=False)
            for j, m in order[OPENED:]:
                for first in range(0, PIECE, SHORT):
                    last = first + SHORT == PIECE
                    gathered(bank[j, m][:, first : first + SHORT], m, j * PIECE + first, start=False, stop=last)
                store(j, m)
